import numpy as np
import ml_dtypes

BF16 = ml_dtypes.bfloat16


def bf(x):
    return np.asarray(x, np.float32).astype(BF16)


def f32(x):
    return np.asarray(x, np.float32)


def f64(x):
    return np.asarray(x).astype(np.float64)


def striped(idx):
    return np.tile(idx.reshape(-1, 16).T, (8, 1))


C, S, K, P, N, M = 1024, 1024, 4, 128, 512, 512


def setup_inputs():
    return {
        'x': f32(np.abs(np.random.standard_normal((C, S)))),
        'dt_w': bf(np.random.standard_normal((C, C)) / np.sqrt(C)),
        'dt_gain': f32(1.0 + 0.1 * np.random.standard_normal((C, 1))),
        'dt_bias': f32(0.1 * np.random.standard_normal((C, 1))),
        'd4_w': bf(np.random.standard_normal((C + C, M)) / np.sqrt(C + C)),
        'd4_gain': f32(1.0 + 0.1 * np.random.standard_normal((M, 1))),
        'd4_bias': f32(0.1 * np.random.standard_normal((M, 1))),
        'offs': striped(np.random.permutation(S)[:N]),
    }


def reference(x, dt_w, dt_gain, dt_bias, d4_w, d4_gain, d4_bias, offs):
    idx = offs[:16].T.reshape(-1)
    pooled = f64(x)[:, idx].reshape(C, P, K).max(axis=-1)
    h = np.maximum((f64(dt_w).T @ pooled) * f64(dt_gain) + f64(dt_bias), 0.0)
    y = f64(d4_w)[:C].T @ h + f64(d4_w)[C:].T @ pooled
    return np.maximum(y * f64(d4_gain) + f64(d4_bias), 0.0)

@@ -1,0 +1,105 @@
+import concourse.mybir as mybir
+from concourse.masks import make_identity
+
+F32 = mybir.dt.float32
+BF16 = mybir.dt.bfloat16
+U16 = mybir.dt.uint16
+COPY = mybir.ActivationFunctionType.Copy
+RELU = mybir.ActivationFunctionType.Relu
+
+P = 128
+CHANNELS = 1024
+POINTS = 1024
+LISTED = 512
+NEIGHBOURS = 4
+SAMPLED = LISTED // NEIGHBOURS
+OUT_CHANNELS = 512
+C_BLOCKS = CHANNELS // P
+O_BLOCKS = OUT_CHANNELS // P
+
+FLOPS = 2 * SAMPLED * (CHANNELS * CHANNELS + 2 * CHANNELS * OUT_CHANNELS)
+
+
+def tile_c3dnet_kernel(tc, x, dt_w, dt_gain, dt_bias, d4_w, d4_gain, d4_bias, offs, out):
+    nc = tc.nc
+    with (
+        tc.tile_pool(name="held", bufs=1) as held,
+        tc.tile_pool(name="ring", bufs=3) as ring,
+        tc.psum_pool(name="psum", bufs=8) as psum,
+    ):
+        offsets = held.tile([P, LISTED // 16], U16, name="offsets")
+        nc.sync.dma_start(offsets[:], offs)
+
+        x_blocks = [held.tile([P, POINTS], F32, name=f"x{i}") for i in range(C_BLOCKS)]
+        dt_rows = [held.tile([P, CHANNELS], BF16, name=f"dt{i}") for i in range(C_BLOCKS)]
+        for i in range(C_BLOCKS):
+            nc.sync.dma_start(x_blocks[i][:], x[i * P : (i + 1) * P, :])
+            nc.sync.dma_start(dt_rows[i][:], dt_w[i * P : (i + 1) * P, :])
+        d4_rows = [held.tile([P, OUT_CHANNELS], BF16, name=f"d4{j}") for j in range(2 * C_BLOCKS)]
+        for j in list(range(C_BLOCKS, 2 * C_BLOCKS)) + list(range(C_BLOCKS)):
+            nc.sync.dma_start(d4_rows[j][:], d4_w[j * P : (j + 1) * P, :])
+
+        vector_rows = held.tile([P, P], F32, name="vector_rows")
+        nc.gpsimd.memset(vector_rows[:], 0.0)
+        first_row = {}
+        row = 0
+        for name, vector in (("dt_gain", dt_gain), ("dt_bias", dt_bias), ("d4_gain", d4_gain), ("d4_bias", d4_bias)):
+            rows = vector.shape[0] // P
+            nc.gpsimd.dma_start(vector_rows[row : row + rows, :], vector.rearrange("(r p) one -> r (p one)", p=P))
+            first_row[name] = row
+            row += rows
+        identity = held.tile([P, P], F32, name="identity")
+        make_identity(nc, identity[:])
+        flipped = psum.tile([P, P], F32, name="flipped", tag="bank")
+        nc.tensor.transpose(flipped[:], vector_rows[:], identity[:])
+        per_channel = held.tile([P, row], F32, name="per_channel")
+        nc.vector.tensor_copy(per_channel[:], flipped[:, 0:row])
+
+        def channel_column(name, block):
+            column = first_row[name] + block
+            return per_channel[:, column : column + 1]
+
+        pooled = [held.tile([P, SAMPLED], BF16, name=f"pooled{i}") for i in range(C_BLOCKS)]
+        h_sums = [psum.tile([P, SAMPLED], F32, name=f"h_sum{m}", tag="bank") for m in range(C_BLOCKS)]
+        for i in range(C_BLOCKS):
+            picked = ring.tile([P, LISTED], F32, name="picked")
+            nc.scalar.activation(picked[:], x_blocks[i][:].indirect(offsets[:]), COPY)
+            with nc.allow_low_precision(reason="a maximum is one of its inputs: the only rounding is the asked one to bfloat16"):
+                nc.vector.tensor_reduce(
+                    pooled[i][:],
+                    picked[:].rearrange("p (n t) -> p n t", t=NEIGHBOURS),
+                    axis=mybir.AxisListType.X,
+                    op=mybir.AluOpType.max,
+                )
+            for m in range(C_BLOCKS):
+                nc.tensor.matmul(
+                    h_sums[m][:],
+                    dt_rows[i][:, m * P : (m + 1) * P],
+                    pooled[i][:],
+                    start=(i == 0),
+                    stop=(i == C_BLOCKS - 1),
+                )
+
+        h = [held.tile([P, SAMPLED], BF16, name=f"h{m}") for m in range(C_BLOCKS)]
+        for m in range(C_BLOCKS):
+            nc.scalar.activation(
+                h[m][:], h_sums[m][:], RELU, bias=channel_column("dt_bias", m), scale=channel_column("dt_gain", m)
+            )
+
+        out_sums = [psum.tile([P, SAMPLED], F32, name=f"out_sum{o}", tag="bank") for o in range(O_BLOCKS)]
+        for i in range(C_BLOCKS):
+            for o in range(O_BLOCKS):
+                nc.tensor.matmul(
+                    out_sums[o][:], d4_rows[C_BLOCKS + i][:, o * P : (o + 1) * P], pooled[i][:], start=(i == 0), stop=False
+                )
+        for i in range(C_BLOCKS):
+            for o in range(O_BLOCKS):
+                nc.tensor.matmul(
+                    out_sums[o][:], d4_rows[i][:, o * P : (o + 1) * P], h[i][:], start=False, stop=(i == C_BLOCKS - 1)
+                )
+        for o in range(O_BLOCKS):
+            result = held.tile([P, SAMPLED], F32, name=f"result{o}")
+            nc.scalar.activation(
+                result[:], out_sums[o][:], RELU, bias=channel_column("d4_bias", o), scale=channel_column("d4_gain", o)
+            )
+            nc.sync.dma_start(out[o * P : (o + 1) * P, :], result[:])

@@ -40,12 +40,12 @@ def tile_c3dnet_kernel(tc, x, dt_w, dt_gain, dt_bias, d4_w, d4_gain, d4_bias, of
             nc.sync.dma_start(d4_rows[j][:], d4_w[j * P : (j + 1) * P, :])
 
         vector_rows = held.tile([P, P], F32, name="vector_rows")
-        nc.gpsimd.memset(vector_rows[:], 0.0)
+        nc.vector.memset(vector_rows[:], 0.0)
         first_row = {}
         row = 0
         for name, vector in (("dt_gain", dt_gain), ("dt_bias", dt_bias), ("d4_gain", d4_gain), ("d4_bias", d4_bias)):
             rows = vector.shape[0] // P
-            nc.gpsimd.dma_start(vector_rows[row : row + rows, :], vector.rearrange("(r p) one -> r (p one)", p=P))
+            nc.scalar.dma_start(vector_rows[row : row + rows, :], vector.rearrange("(r p) one -> r (p one)", p=P))
             first_row[name] = row
             row += rows
         identity = held.tile([P, P], F32, name="identity")

@@ -1,5 +1,4 @@
 import concourse.mybir as mybir
-from concourse.masks import make_identity
 
 F32 = mybir.dt.float32
 BF16 = mybir.dt.bfloat16
@@ -14,8 +13,13 @@ LISTED = 512
 NEIGHBOURS = 4
 SAMPLED = LISTED // NEIGHBOURS
 OUT_CHANNELS = 512
-C_BLOCKS = CHANNELS // P
-O_BLOCKS = OUT_CHANNELS // P
+SLOTS = CHANNELS // P
+OUT_SLOTS = OUT_CHANNELS // P
+BANK = 512
+PER_BANK = BANK // SAMPLED
+DT_PIECE = 2
+D4_POOLED_PIECE = 4
+D4_H_PIECE = 2
 
 FLOPS = 2 * SAMPLED * (CHANNELS * CHANNELS + 2 * CHANNELS * OUT_CHANNELS)
 
@@ -25,81 +29,109 @@ def tile_c3dnet_kernel(tc, x, dt_w, dt_gain, dt_bias, d4_w, d4_gain, d4_bias, of
     with (
         tc.tile_pool(name="held", bufs=1) as held,
         tc.tile_pool(name="ring", bufs=3) as ring,
-        tc.psum_pool(name="psum", bufs=8) as psum,
+        tc.psum_pool(name="psum", bufs=1) as psum,
     ):
         offsets = held.tile([P, LISTED // 16], U16, name="offsets")
         nc.sync.dma_start(offsets[:], offs)
 
-        x_blocks = [held.tile([P, POINTS], F32, name=f"x{i}") for i in range(C_BLOCKS)]
-        dt_rows = [held.tile([P, CHANNELS], BF16, name=f"dt{i}") for i in range(C_BLOCKS)]
-        for i in range(C_BLOCKS):
-            nc.sync.dma_start(x_blocks[i][:], x[i * P : (i + 1) * P, :])
-            nc.sync.dma_start(dt_rows[i][:], dt_w[i * P : (i + 1) * P, :])
-        d4_rows = [held.tile([P, OUT_CHANNELS], BF16, name=f"d4{j}") for j in range(2 * C_BLOCKS)]
-        for j in list(range(C_BLOCKS, 2 * C_BLOCKS)) + list(range(C_BLOCKS)):
-            nc.sync.dma_start(d4_rows[j][:], d4_w[j * P : (j + 1) * P, :])
+        x_by_slot = x.rearrange("(p r) s -> p r s", r=SLOTS)
+        dt_by_slot = dt_w.rearrange("(p r) m -> p r m", r=SLOTS)
+        d4_h_by_slot = d4_w[0:CHANNELS, :].rearrange("(p r) o -> p r o", r=SLOTS)
+        d4_pooled_by_slot = d4_w[CHANNELS : 2 * CHANNELS, :].rearrange("(p r) o -> p r o", r=SLOTS)
 
-        vector_rows = held.tile([P, P], F32, name="vector_rows")
-        nc.vector.memset(vector_rows[:], 0.0)
-        first_row = {}
-        row = 0
-        for name, vector in (("dt_gain", dt_gain), ("dt_bias", dt_bias), ("d4_gain", d4_gain), ("d4_bias", d4_bias)):
-            rows = vector.shape[0] // P
-            nc.scalar.dma_start(vector_rows[row : row + rows, :], vector.rearrange("(r p) one -> r (p one)", p=P))
-            first_row[name] = row
-            row += rows
-        identity = held.tile([P, P], F32, name="identity")
-        make_identity(nc, identity[:])
-        flipped = psum.tile([P, P], F32, name="flipped", tag="bank")
-        nc.tensor.transpose(flipped[:], vector_rows[:], identity[:])
-        per_channel = held.tile([P, row], F32, name="per_channel")
-        nc.vector.tensor_copy(per_channel[:], flipped[:, 0:row])
+        x_slots = [held.tile([P, POINTS], F32, name=f"x{r}") for r in range(SLOTS)]
+        dt_pieces = [held.tile([P, DT_PIECE, CHANNELS], BF16, name=f"dt{k}") for k in range(SLOTS // DT_PIECE)]
+        for k in range(SLOTS // DT_PIECE):
+            for r in range(k * DT_PIECE, (k + 1) * DT_PIECE):
+                nc.sync.dma_start(x_slots[r][:], x_by_slot[:, r, :])
+            nc.sync.dma_start(dt_pieces[k][:], dt_by_slot[:, k * DT_PIECE : (k + 1) * DT_PIECE, :])
+        d4_pooled_pieces = [
+            held.tile([P, D4_POOLED_PIECE, OUT_CHANNELS], BF16, name=f"d4_pooled{k}")
+            for k in range(SLOTS // D4_POOLED_PIECE)
+        ]
+        for k in range(SLOTS // D4_POOLED_PIECE):
+            nc.sync.dma_start(
+                d4_pooled_pieces[k][:], d4_pooled_by_slot[:, k * D4_POOLED_PIECE : (k + 1) * D4_POOLED_PIECE, :]
+            )
+        d4_h_pieces = [
+            held.tile([P, D4_H_PIECE, OUT_CHANNELS], BF16, name=f"d4_h{k}") for k in range(SLOTS // D4_H_PIECE)
+        ]
+        for k in range(SLOTS // D4_H_PIECE):
+            nc.sync.dma_start(d4_h_pieces[k][:], d4_h_by_slot[:, k * D4_H_PIECE : (k + 1) * D4_H_PIECE, :])
 
-        def channel_column(name, block):
-            column = first_row[name] + block
-            return per_channel[:, column : column + 1]
+        def every_nth_column(rows, step, first):
+            return rows.rearrange("p (m r) -> p r m", r=step)[:, first, :]
 
-        pooled = [held.tile([P, SAMPLED], BF16, name=f"pooled{i}") for i in range(C_BLOCKS)]
-        h_sums = [psum.tile([P, SAMPLED], F32, name=f"h_sum{m}", tag="bank") for m in range(C_BLOCKS)]
-        for i in range(C_BLOCKS):
+        def dt_weights(r_in, r_out):
+            return every_nth_column(dt_pieces[r_in // DT_PIECE][:, r_in % DT_PIECE, :], SLOTS, r_out)
+
+        def d4_pooled_weights(r_in, q_out):
+            rows = d4_pooled_pieces[r_in // D4_POOLED_PIECE][:, r_in % D4_POOLED_PIECE, :]
+            return every_nth_column(rows, OUT_SLOTS, q_out)
+
+        def d4_h_weights(r_in, q_out):
+            return every_nth_column(d4_h_pieces[r_in // D4_H_PIECE][:, r_in % D4_H_PIECE, :], OUT_SLOTS, q_out)
+
+        dt_gains = held.tile([P, SLOTS], F32, name="dt_gains")
+        dt_biases = held.tile([P, SLOTS], F32, name="dt_biases")
+        d4_gains = held.tile([P, OUT_SLOTS], F32, name="d4_gains")
+        d4_biases = held.tile([P, OUT_SLOTS], F32, name="d4_biases")
+        for columns, vector in ((dt_gains, dt_gain), (dt_biases, dt_bias), (d4_gains, d4_gain), (d4_biases, d4_bias)):
+            nc.gpsimd.dma_start(columns[:], vector.rearrange("(p r) one -> p (r one)", p=P))
+
+        zero_weights = held.tile([P, P], BF16, name="zero_weights")
+        zero_columns = held.tile([P, BANK], BF16, name="zero_columns")
+        nc.vector.memset(zero_weights[:], 0.0)
+        nc.vector.memset(zero_columns[:], 0.0)
+        h_banks = [psum.tile([P, BANK], F32, name=f"h_bank{b}") for b in range(SLOTS // PER_BANK)]
+        out_bank = psum.tile([P, BANK], F32, name="out_bank")
+        for bank in h_banks + [out_bank]:
+            nc.tensor.matmul(bank[:], zero_weights[:], zero_columns[:], start=True, stop=False)
+
+        def h_sum(r):
+            return h_banks[r // PER_BANK][:, (r % PER_BANK) * SAMPLED : (r % PER_BANK + 1) * SAMPLED]
+
+        def out_sum(q):
+            return out_bank[:, q * SAMPLED : (q + 1) * SAMPLED]
+
+        pooled = [held.tile([P, SAMPLED], BF16, name=f"pooled{r}") for r in range(SLOTS)]
+        for r_in in range(SLOTS):
             picked = ring.tile([P, LISTED], F32, name="picked")
-            nc.scalar.activation(picked[:], x_blocks[i][:].indirect(offsets[:]), COPY)
+            nc.scalar.activation(picked[:], x_slots[r_in][:].indirect(offsets[:]), COPY)
             with nc.allow_low_precision(reason="a maximum is one of its inputs: the only rounding is the asked one to bfloat16"):
                 nc.vector.tensor_reduce(
-                    pooled[i][:],
+                    pooled[r_in][:],
                     picked[:].rearrange("p (n t) -> p n t", t=NEIGHBOURS),
                     axis=mybir.AxisListType.X,
                     op=mybir.AluOpType.max,
                 )
-            for m in range(C_BLOCKS):
+            for r_out in range(SLOTS):
                 nc.tensor.matmul(
-                    h_sums[m][:],
-                    dt_rows[i][:, m * P : (m + 1) * P],
-                    pooled[i][:],
-                    start=(i == 0),
-                    stop=(i == C_BLOCKS - 1),
+                    h_sum(r_out),
+                    dt_weights(r_in, r_out),
+                    pooled[r_in][:],
+                    start=False,
+                    stop=(r_in == SLOTS - 1 and r_out % PER_BANK == PER_BANK - 1),
                 )
 
-        h = [held.tile([P, SAMPLED], BF16, name=f"h{m}") for m in range(C_BLOCKS)]
-        for m in range(C_BLOCKS):
-            nc.scalar.activation(
-                h[m][:], h_sums[m][:], RELU, bias=channel_column("dt_bias", m), scale=channel_column("dt_gain", m)
-            )
-
-        out_sums = [psum.tile([P, SAMPLED], F32, name=f"out_sum{o}", tag="bank") for o in range(O_BLOCKS)]
-        for i in range(C_BLOCKS):
-            for o in range(O_BLOCKS):
+        for r_in in range(SLOTS):
+            for q_out in range(OUT_SLOTS):
+                nc.tensor.matmul(out_sum(q_out), d4_pooled_weights(r_in, q_out), pooled[r_in][:], start=False, stop=False)
+        h = [held.tile([P, SAMPLED], BF16, name=f"h{r}") for r in range(SLOTS)]
+        for r in range(SLOTS):
+            nc.scalar.activation(h[r][:], h_sum(r), RELU, bias=dt_biases[:, r : r + 1], scale=dt_gains[:, r : r + 1])
+        for r_in in range(SLOTS):
+            for q_out in range(OUT_SLOTS):
                 nc.tensor.matmul(
-                    out_sums[o][:], d4_rows[C_BLOCKS + i][:, o * P : (o + 1) * P], pooled[i][:], start=(i == 0), stop=False
+                    out_sum(q_out),
+                    d4_h_weights(r_in, q_out),
+                    h[r_in][:],
+                    start=False,
+                    stop=(r_in == SLOTS - 1 and q_out == OUT_SLOTS - 1),
                 )
-        for i in range(C_BLOCKS):
-            for o in range(O_BLOCKS):
-                nc.tensor.matmul(
-                    out_sums[o][:], d4_rows[i][:, o * P : (o + 1) * P], h[i][:], start=False, stop=(i == C_BLOCKS - 1)
-                )
-        for o in range(O_BLOCKS):
-            result = held.tile([P, SAMPLED], F32, name=f"result{o}")
+        result = held.tile([P, OUT_SLOTS, SAMPLED], F32, name="result")
+        for q in range(OUT_SLOTS):
             nc.scalar.activation(
-                result[:], out_sums[o][:], RELU, bias=channel_column("d4_bias", o), scale=channel_column("d4_gain", o)
+                result[:, q, :], out_sum(q), RELU, bias=d4_biases[:, q : q + 1], scale=d4_gains[:, q : q + 1]
             )
-            nc.sync.dma_start(out[o * P : (o + 1) * P, :], result[:])
+        nc.sync.dma_start(out.rearrange("(p q) n -> p q n", q=OUT_SLOTS), result[:])

@@ -40,10 +40,10 @@ def tile_c3dnet_kernel(tc, x, dt_w, dt_gain, dt_bias, d4_w, d4_gain, d4_bias, of
         d4_pooled_by_slot = d4_w[CHANNELS : 2 * CHANNELS, :].rearrange("(p r) o -> p r o", r=SLOTS)
 
         x_slots = [held.tile([P, POINTS], F32, name=f"x{r}") for r in range(SLOTS)]
+        for r in range(SLOTS):
+            nc.sync.dma_start(x_slots[r][:], x_by_slot[:, r, :])
         dt_pieces = [held.tile([P, DT_PIECE, CHANNELS], BF16, name=f"dt{k}") for k in range(SLOTS // DT_PIECE)]
         for k in range(SLOTS // DT_PIECE):
-            for r in range(k * DT_PIECE, (k + 1) * DT_PIECE):
-                nc.sync.dma_start(x_slots[r][:], x_by_slot[:, r, :])
             nc.sync.dma_start(dt_pieces[k][:], dt_by_slot[:, k * DT_PIECE : (k + 1) * DT_PIECE, :])
         d4_pooled_pieces = [
             held.tile([P, D4_POOLED_PIECE, OUT_CHANNELS], BF16, name=f"d4_pooled{k}")
@@ -79,14 +79,12 @@ def tile_c3dnet_kernel(tc, x, dt_w, dt_gain, dt_bias, d4_w, d4_gain, d4_bias, of
         for columns, vector in ((dt_gains, dt_gain), (dt_biases, dt_bias), (d4_gains, d4_gain), (d4_biases, d4_bias)):
             nc.gpsimd.dma_start(columns[:], vector.rearrange("(p r) one -> p (r one)", p=P))
 
-        zero_weights = held.tile([P, P], BF16, name="zero_weights")
-        zero_columns = held.tile([P, BANK], BF16, name="zero_columns")
-        nc.vector.memset(zero_weights[:], 0.0)
-        nc.vector.memset(zero_columns[:], 0.0)
+        zeros = held.tile([P, BANK], BF16, name="zeros")
+        nc.scalar.memzero(zeros[:])
         h_banks = [psum.tile([P, BANK], F32, name=f"h_bank{b}") for b in range(SLOTS // PER_BANK)]
         out_bank = psum.tile([P, BANK], F32, name="out_bank")
         for bank in h_banks + [out_bank]:
-            nc.tensor.matmul(bank[:], zero_weights[:], zero_columns[:], start=True, stop=False)
+            nc.tensor.matmul(bank[:], zeros[:, 0:P], zeros[:], start=True, stop=False)
 
         def h_sum(r):
             return h_banks[r // PER_BANK][:, (r % PER_BANK) * SAMPLED : (r % PER_BANK + 1) * SAMPLED]

@@ -40,10 +40,10 @@ def tile_c3dnet_kernel(tc, x, dt_w, dt_gain, dt_bias, d4_w, d4_gain, d4_bias, of
         d4_pooled_by_slot = d4_w[CHANNELS : 2 * CHANNELS, :].rearrange("(p r) o -> p r o", r=SLOTS)
 
         x_slots = [held.tile([P, POINTS], F32, name=f"x{r}") for r in range(SLOTS)]
-        for r in range(SLOTS):
-            nc.sync.dma_start(x_slots[r][:], x_by_slot[:, r, :])
         dt_pieces = [held.tile([P, DT_PIECE, CHANNELS], BF16, name=f"dt{k}") for k in range(SLOTS // DT_PIECE)]
         for k in range(SLOTS // DT_PIECE):
+            for r in range(k * DT_PIECE, (k + 1) * DT_PIECE):
+                nc.sync.dma_start(x_slots[r][:], x_by_slot[:, r, :])
             nc.sync.dma_start(dt_pieces[k][:], dt_by_slot[:, k * DT_PIECE : (k + 1) * DT_PIECE, :])
         d4_pooled_pieces = [
             held.tile([P, D4_POOLED_PIECE, OUT_CHANNELS], BF16, name=f"d4_pooled{k}")
@@ -82,15 +82,13 @@ def tile_c3dnet_kernel(tc, x, dt_w, dt_gain, dt_bias, d4_w, d4_gain, d4_bias, of
         zeros = held.tile([P, BANK], BF16, name="zeros")
         nc.scalar.memzero(zeros[:])
         h_banks = [psum.tile([P, BANK], F32, name=f"h_bank{b}") for b in range(SLOTS // PER_BANK)]
-        out_bank = psum.tile([P, BANK], F32, name="out_bank")
-        for bank in h_banks + [out_bank]:
+        for bank in h_banks:
             nc.tensor.matmul(bank[:], zeros[:, 0:P], zeros[:], start=True, stop=False)
 
         def h_sum(r):
             return h_banks[r // PER_BANK][:, (r % PER_BANK) * SAMPLED : (r % PER_BANK + 1) * SAMPLED]
 
-        def out_sum(q):
-            return out_bank[:, q * SAMPLED : (q + 1) * SAMPLED]
+        out_sums = [psum.tile([P, SAMPLED], F32, name=f"out_sum{q}") for q in range(OUT_SLOTS)]
 
         pooled = [held.tile([P, SAMPLED], BF16, name=f"pooled{r}") for r in range(SLOTS)]
         for r_in in range(SLOTS):
@@ -114,22 +112,27 @@ def tile_c3dnet_kernel(tc, x, dt_w, dt_gain, dt_bias, d4_w, d4_gain, d4_bias, of
 
         for r_in in range(SLOTS):
             for q_out in range(OUT_SLOTS):
-                nc.tensor.matmul(out_sum(q_out), d4_pooled_weights(r_in, q_out), pooled[r_in][:], start=False, stop=False)
+                nc.tensor.matmul(
+                    out_sums[q_out][:], d4_pooled_weights(r_in, q_out), pooled[r_in][:], start=(r_in == 0), stop=False
+                )
         h = [held.tile([P, SAMPLED], BF16, name=f"h{r}") for r in range(SLOTS)]
         for r in range(SLOTS):
             nc.scalar.activation(h[r][:], h_sum(r), RELU, bias=dt_biases[:, r : r + 1], scale=dt_gains[:, r : r + 1])
-        for r_in in range(SLOTS):
+        for k in range(SLOTS // D4_H_PIECE):
             for q_out in range(OUT_SLOTS):
-                nc.tensor.matmul(
-                    out_sum(q_out),
-                    d4_h_weights(r_in, q_out),
-                    h[r_in][:],
-                    start=False,
-                    stop=(r_in == SLOTS - 1 and q_out == OUT_SLOTS - 1),
-                )
+                for r_in in range(k * D4_H_PIECE, (k + 1) * D4_H_PIECE):
+                    nc.tensor.matmul(
+                        out_sums[q_out][:], d4_h_weights(r_in, q_out), h[r_in][:], start=False, stop=(r_in == SLOTS - 1)
+                    )
+        out_by_slot = out.rearrange("(p q) n -> p q n", q=OUT_SLOTS)
         result = held.tile([P, OUT_SLOTS, SAMPLED], F32, name="result")
         for q in range(OUT_SLOTS):
-            nc.scalar.activation(
-                result[:, q, :], out_sum(q), RELU, bias=d4_biases[:, q : q + 1], scale=d4_gains[:, q : q + 1]
-            )
-        nc.sync.dma_start(out.rearrange("(p q) n -> p q n", q=OUT_SLOTS), result[:])
+            gain, bias = d4_gains[:, q : q + 1], d4_biases[:, q : q + 1]
+            if q % 2 == 0:
+                nc.scalar.activation(result[:, q, :], out_sums[q][:], RELU, bias=bias, scale=gain)
+            else:
+                nc.vector.tensor_scalar(
+                    result[:, q, :], out_sums[q][:], gain, bias, op0=mybir.AluOpType.mult, op1=mybir.AluOpType.add
+                )
+                nc.vector.tensor_scalar_max(result[:, q, :], result[:, q, :], 0.0)
+            nc.sync.dma_start(out_by_slot[:, q, :], result[:, q, :])

@@ -17,9 +17,8 @@ SLOTS = CHANNELS // P
 OUT_SLOTS = OUT_CHANNELS // P
 BANK = 512
 PER_BANK = BANK // SAMPLED
-DT_PIECE = 2
-D4_POOLED_PIECE = 4
-D4_H_PIECE = 2
+PIECE = 2
+PIECES = SLOTS // PIECE
 
 FLOPS = 2 * SAMPLED * (CHANNELS * CHANNELS + 2 * CHANNELS * OUT_CHANNELS)
 
@@ -40,37 +39,29 @@ def tile_c3dnet_kernel(tc, x, dt_w, dt_gain, dt_bias, d4_w, d4_gain, d4_bias, of
         d4_pooled_by_slot = d4_w[CHANNELS : 2 * CHANNELS, :].rearrange("(p r) o -> p r o", r=SLOTS)
 
         x_slots = [held.tile([P, POINTS], F32, name=f"x{r}") for r in range(SLOTS)]
-        dt_pieces = [held.tile([P, DT_PIECE, CHANNELS], BF16, name=f"dt{k}") for k in range(SLOTS // DT_PIECE)]
-        for k in range(SLOTS // DT_PIECE):
-            for r in range(k * DT_PIECE, (k + 1) * DT_PIECE):
+        dt_pieces = [held.tile([P, PIECE, CHANNELS], BF16, name=f"dt{k}") for k in range(PIECES)]
+        d4_pooled_pieces = [held.tile([P, PIECE, OUT_CHANNELS], BF16, name=f"d4_pooled{k}") for k in range(PIECES)]
+        d4_h_pieces = [held.tile([P, PIECE, OUT_CHANNELS], BF16, name=f"d4_h{k}") for k in range(PIECES)]
+        for k in range(PIECES):
+            in_piece = slice(k * PIECE, (k + 1) * PIECE)
+            for r in range(k * PIECE, (k + 1) * PIECE):
                 nc.sync.dma_start(x_slots[r][:], x_by_slot[:, r, :])
-            nc.sync.dma_start(dt_pieces[k][:], dt_by_slot[:, k * DT_PIECE : (k + 1) * DT_PIECE, :])
-        d4_pooled_pieces = [
-            held.tile([P, D4_POOLED_PIECE, OUT_CHANNELS], BF16, name=f"d4_pooled{k}")
-            for k in range(SLOTS // D4_POOLED_PIECE)
-        ]
-        for k in range(SLOTS // D4_POOLED_PIECE):
-            nc.sync.dma_start(
-                d4_pooled_pieces[k][:], d4_pooled_by_slot[:, k * D4_POOLED_PIECE : (k + 1) * D4_POOLED_PIECE, :]
-            )
-        d4_h_pieces = [
-            held.tile([P, D4_H_PIECE, OUT_CHANNELS], BF16, name=f"d4_h{k}") for k in range(SLOTS // D4_H_PIECE)
-        ]
-        for k in range(SLOTS // D4_H_PIECE):
-            nc.sync.dma_start(d4_h_pieces[k][:], d4_h_by_slot[:, k * D4_H_PIECE : (k + 1) * D4_H_PIECE, :])
+            nc.sync.dma_start(dt_pieces[k][:], dt_by_slot[:, in_piece, :])
+            nc.sync.dma_start(d4_pooled_pieces[k][:], d4_pooled_by_slot[:, in_piece, :])
+        for k in range(PIECES):
+            nc.sync.dma_start(d4_h_pieces[k][:], d4_h_by_slot[:, k * PIECE : (k + 1) * PIECE, :])
 
         def every_nth_column(rows, step, first):
             return rows.rearrange("p (m r) -> p r m", r=step)[:, first, :]
 
         def dt_weights(r_in, r_out):
-            return every_nth_column(dt_pieces[r_in // DT_PIECE][:, r_in % DT_PIECE, :], SLOTS, r_out)
+            return every_nth_column(dt_pieces[r_in // PIECE][:, r_in % PIECE, :], SLOTS, r_out)
 
         def d4_pooled_weights(r_in, q_out):
-            rows = d4_pooled_pieces[r_in // D4_POOLED_PIECE][:, r_in % D4_POOLED_PIECE, :]
-            return every_nth_column(rows, OUT_SLOTS, q_out)
+            return every_nth_column(d4_pooled_pieces[r_in // PIECE][:, r_in % PIECE, :], OUT_SLOTS, q_out)
 
         def d4_h_weights(r_in, q_out):
-            return every_nth_column(d4_h_pieces[r_in // D4_H_PIECE][:, r_in % D4_H_PIECE, :], OUT_SLOTS, q_out)
+            return every_nth_column(d4_h_pieces[r_in // PIECE][:, r_in % PIECE, :], OUT_SLOTS, q_out)
 
         dt_gains = held.tile([P, SLOTS], F32, name="dt_gains")
         dt_biases = held.tile([P, SLOTS], F32, name="dt_biases")
@@ -109,18 +100,17 @@ def tile_c3dnet_kernel(tc, x, dt_w, dt_gain, dt_bias, d4_w, d4_gain, d4_bias, of
                     start=False,
                     stop=(r_in == SLOTS - 1 and r_out % PER_BANK == PER_BANK - 1),
                 )
-
-        for r_in in range(SLOTS):
             for q_out in range(OUT_SLOTS):
                 nc.tensor.matmul(
                     out_sums[q_out][:], d4_pooled_weights(r_in, q_out), pooled[r_in][:], start=(r_in == 0), stop=False
                 )
+
         h = [held.tile([P, SAMPLED], BF16, name=f"h{r}") for r in range(SLOTS)]
         for r in range(SLOTS):
             nc.scalar.activation(h[r][:], h_sum(r), RELU, bias=dt_biases[:, r : r + 1], scale=dt_gains[:, r : r + 1])
-        for k in range(SLOTS // D4_H_PIECE):
+        for k in range(PIECES):
             for q_out in range(OUT_SLOTS):
-                for r_in in range(k * D4_H_PIECE, (k + 1) * D4_H_PIECE):
+                for r_in in range(k * PIECE, (k + 1) * PIECE):
                     nc.tensor.matmul(
                         out_sums[q_out][:], d4_h_weights(r_in, q_out), h[r_in][:], start=False, stop=(r_in == SLOTS - 1)
                     )

@@ -17,8 +17,9 @@ SLOTS = CHANNELS // P
 OUT_SLOTS = OUT_CHANNELS // P
 BANK = 512
 PER_BANK = BANK // SAMPLED
-PIECE = 2
-PIECES = SLOTS // PIECE
+DT_PIECE = 2
+D4_POOLED_PIECE = 4
+D4_H_PIECE = 2
 
 FLOPS = 2 * SAMPLED * (CHANNELS * CHANNELS + 2 * CHANNELS * OUT_CHANNELS)
 
@@ -39,29 +40,46 @@ def tile_c3dnet_kernel(tc, x, dt_w, dt_gain, dt_bias, d4_w, d4_gain, d4_bias, of
         d4_pooled_by_slot = d4_w[CHANNELS : 2 * CHANNELS, :].rearrange("(p r) o -> p r o", r=SLOTS)
 
         x_slots = [held.tile([P, POINTS], F32, name=f"x{r}") for r in range(SLOTS)]
-        dt_pieces = [held.tile([P, PIECE, CHANNELS], BF16, name=f"dt{k}") for k in range(PIECES)]
-        d4_pooled_pieces = [held.tile([P, PIECE, OUT_CHANNELS], BF16, name=f"d4_pooled{k}") for k in range(PIECES)]
-        d4_h_pieces = [held.tile([P, PIECE, OUT_CHANNELS], BF16, name=f"d4_h{k}") for k in range(PIECES)]
-        for k in range(PIECES):
-            in_piece = slice(k * PIECE, (k + 1) * PIECE)
-            for r in range(k * PIECE, (k + 1) * PIECE):
-                nc.sync.dma_start(x_slots[r][:], x_by_slot[:, r, :])
-            nc.sync.dma_start(dt_pieces[k][:], dt_by_slot[:, in_piece, :])
-            nc.sync.dma_start(d4_pooled_pieces[k][:], d4_pooled_by_slot[:, in_piece, :])
-        for k in range(PIECES):
-            nc.sync.dma_start(d4_h_pieces[k][:], d4_h_by_slot[:, k * PIECE : (k + 1) * PIECE, :])
+        dt_pieces = [held.tile([P, DT_PIECE, CHANNELS], BF16, name=f"dt{k}") for k in range(SLOTS // DT_PIECE)]
+
+        def load_x(r):
+            nc.sync.dma_start(x_slots[r][:], x_by_slot[:, r, :])
+
+        def load_dt(k):
+            nc.sync.dma_start(dt_pieces[k][:], dt_by_slot[:, k * DT_PIECE : (k + 1) * DT_PIECE, :])
+
+        for r in range(SLOTS - 1):
+            load_x(r)
+        for k in range(SLOTS // DT_PIECE - 1):
+            load_dt(k)
+        load_x(SLOTS - 1)
+        load_dt(SLOTS // DT_PIECE - 1)
+        d4_pooled_pieces = [
+            held.tile([P, D4_POOLED_PIECE, OUT_CHANNELS], BF16, name=f"d4_pooled{k}")
+            for k in range(SLOTS // D4_POOLED_PIECE)
+        ]
+        for k in range(SLOTS // D4_POOLED_PIECE):
+            nc.sync.dma_start(
+                d4_pooled_pieces[k][:], d4_pooled_by_slot[:, k * D4_POOLED_PIECE : (k + 1) * D4_POOLED_PIECE, :]
+            )
+        d4_h_pieces = [
+            held.tile([P, D4_H_PIECE, OUT_CHANNELS], BF16, name=f"d4_h{k}") for k in range(SLOTS // D4_H_PIECE)
+        ]
+        for k in range(SLOTS // D4_H_PIECE):
+            nc.sync.dma_start(d4_h_pieces[k][:], d4_h_by_slot[:, k * D4_H_PIECE : (k + 1) * D4_H_PIECE, :])
 
         def every_nth_column(rows, step, first):
             return rows.rearrange("p (m r) -> p r m", r=step)[:, first, :]
 
         def dt_weights(r_in, r_out):
-            return every_nth_column(dt_pieces[r_in // PIECE][:, r_in % PIECE, :], SLOTS, r_out)
+            return every_nth_column(dt_pieces[r_in // DT_PIECE][:, r_in % DT_PIECE, :], SLOTS, r_out)
 
         def d4_pooled_weights(r_in, q_out):
-            return every_nth_column(d4_pooled_pieces[r_in // PIECE][:, r_in % PIECE, :], OUT_SLOTS, q_out)
+            rows = d4_pooled_pieces[r_in // D4_POOLED_PIECE][:, r_in % D4_POOLED_PIECE, :]
+            return every_nth_column(rows, OUT_SLOTS, q_out)
 
         def d4_h_weights(r_in, q_out):
-            return every_nth_column(d4_h_pieces[r_in // PIECE][:, r_in % PIECE, :], OUT_SLOTS, q_out)
+            return every_nth_column(d4_h_pieces[r_in // D4_H_PIECE][:, r_in % D4_H_PIECE, :], OUT_SLOTS, q_out)
 
         dt_gains = held.tile([P, SLOTS], F32, name="dt_gains")
         dt_biases = held.tile([P, SLOTS], F32, name="dt_biases")
@@ -100,17 +118,18 @@ def tile_c3dnet_kernel(tc, x, dt_w, dt_gain, dt_bias, d4_w, d4_gain, d4_bias, of
                     start=False,
                     stop=(r_in == SLOTS - 1 and r_out % PER_BANK == PER_BANK - 1),
                 )
+
+        for r_in in range(SLOTS):
             for q_out in range(OUT_SLOTS):
                 nc.tensor.matmul(
                     out_sums[q_out][:], d4_pooled_weights(r_in, q_out), pooled[r_in][:], start=(r_in == 0), stop=False
                 )
-
         h = [held.tile([P, SAMPLED], BF16, name=f"h{r}") for r in range(SLOTS)]
         for r in range(SLOTS):
             nc.scalar.activation(h[r][:], h_sum(r), RELU, bias=dt_biases[:, r : r + 1], scale=dt_gains[:, r : r + 1])
-        for k in range(PIECES):
+        for k in range(SLOTS // D4_H_PIECE):
             for q_out in range(OUT_SLOTS):
-                for r_in in range(k * PIECE, (k + 1) * PIECE):
+                for r_in in range(k * D4_H_PIECE, (k + 1) * D4_H_PIECE):
                     nc.tensor.matmul(
                         out_sums[q_out][:], d4_h_weights(r_in, q_out), h[r_in][:], start=False, stop=(r_in == SLOTS - 1)
                     )

@@ -17,9 +17,10 @@ SLOTS = CHANNELS // P
 OUT_SLOTS = OUT_CHANNELS // P
 BANK = 512
 PER_BANK = BANK // SAMPLED
+X_PIECE = 2
 DT_PIECE = 2
 D4_POOLED_PIECE = 4
-D4_H_PIECE = 2
+D4_H_PIECE = 4
 
 FLOPS = 2 * SAMPLED * (CHANNELS * CHANNELS + 2 * CHANNELS * OUT_CHANNELS)
 
@@ -32,41 +33,49 @@ def tile_c3dnet_kernel(tc, x, dt_w, dt_gain, dt_bias, d4_w, d4_gain, d4_bias, of
         tc.psum_pool(name="psum", bufs=1) as psum,
     ):
         offsets = held.tile([P, LISTED // 16], U16, name="offsets")
-        nc.sync.dma_start(offsets[:], offs)
 
         x_by_slot = x.rearrange("(p r) s -> p r s", r=SLOTS)
         dt_by_slot = dt_w.rearrange("(p r) m -> p r m", r=SLOTS)
         d4_h_by_slot = d4_w[0:CHANNELS, :].rearrange("(p r) o -> p r o", r=SLOTS)
         d4_pooled_by_slot = d4_w[CHANNELS : 2 * CHANNELS, :].rearrange("(p r) o -> p r o", r=SLOTS)
 
-        x_slots = [held.tile([P, POINTS], F32, name=f"x{r}") for r in range(SLOTS)]
+        x_pieces = [held.tile([P, X_PIECE, POINTS], F32, name=f"x{k}") for k in range(SLOTS // X_PIECE)]
         dt_pieces = [held.tile([P, DT_PIECE, CHANNELS], BF16, name=f"dt{k}") for k in range(SLOTS // DT_PIECE)]
-
-        def load_x(r):
-            nc.sync.dma_start(x_slots[r][:], x_by_slot[:, r, :])
-
-        def load_dt(k):
-            nc.sync.dma_start(dt_pieces[k][:], dt_by_slot[:, k * DT_PIECE : (k + 1) * DT_PIECE, :])
-
-        for r in range(SLOTS - 1):
-            load_x(r)
-        for k in range(SLOTS // DT_PIECE - 1):
-            load_dt(k)
-        load_x(SLOTS - 1)
-        load_dt(SLOTS // DT_PIECE - 1)
         d4_pooled_pieces = [
             held.tile([P, D4_POOLED_PIECE, OUT_CHANNELS], BF16, name=f"d4_pooled{k}")
             for k in range(SLOTS // D4_POOLED_PIECE)
         ]
-        for k in range(SLOTS // D4_POOLED_PIECE):
-            nc.sync.dma_start(
-                d4_pooled_pieces[k][:], d4_pooled_by_slot[:, k * D4_POOLED_PIECE : (k + 1) * D4_POOLED_PIECE, :]
-            )
         d4_h_pieces = [
             held.tile([P, D4_H_PIECE, OUT_CHANNELS], BF16, name=f"d4_h{k}") for k in range(SLOTS // D4_H_PIECE)
         ]
-        for k in range(SLOTS // D4_H_PIECE):
+
+        def load_x(k):
+            nc.sync.dma_start(x_pieces[k][:], x_by_slot[:, k * X_PIECE : (k + 1) * X_PIECE, :])
+
+        def load_dt(k):
+            nc.sync.dma_start(dt_pieces[k][:], dt_by_slot[:, k * DT_PIECE : (k + 1) * DT_PIECE, :])
+
+        def load_d4_pooled(k):
+            nc.sync.dma_start(
+                d4_pooled_pieces[k][:], d4_pooled_by_slot[:, k * D4_POOLED_PIECE : (k + 1) * D4_POOLED_PIECE, :]
+            )
+
+        def load_d4_h(k):
             nc.sync.dma_start(d4_h_pieces[k][:], d4_h_by_slot[:, k * D4_H_PIECE : (k + 1) * D4_H_PIECE, :])
+
+        load_x(0)
+        nc.sync.dma_start(offsets[:], offs)
+        load_x(1)
+        load_x(2)
+        load_dt(0)
+        load_dt(1)
+        load_d4_pooled(0)
+        load_x(3)
+        load_dt(2)
+        load_dt(3)
+        load_d4_pooled(1)
+        load_d4_h(0)
+        load_d4_h(1)
 
         def every_nth_column(rows, step, first):
             return rows.rearrange("p (m r) -> p r m", r=step)[:, first, :]
@@ -100,16 +109,19 @@ def tile_c3dnet_kernel(tc, x, dt_w, dt_gain, dt_bias, d4_w, d4_gain, d4_bias, of
         out_sums = [psum.tile([P, SAMPLED], F32, name=f"out_sum{q}") for q in range(OUT_SLOTS)]
 
         pooled = [held.tile([P, SAMPLED], BF16, name=f"pooled{r}") for r in range(SLOTS)]
-        for r_in in range(SLOTS):
+
+        def pool(r):
             picked = ring.tile([P, LISTED], F32, name="picked")
-            nc.scalar.activation(picked[:], x_slots[r_in][:].indirect(offsets[:]), COPY)
+            nc.scalar.activation(picked[:], x_pieces[r // X_PIECE][:, r % X_PIECE, :].indirect(offsets[:]), COPY)
             with nc.allow_low_precision(reason="a maximum is one of its inputs: the only rounding is the asked one to bfloat16"):
                 nc.vector.tensor_reduce(
-                    pooled[r_in][:],
+                    pooled[r][:],
                     picked[:].rearrange("p (n t) -> p n t", t=NEIGHBOURS),
                     axis=mybir.AxisListType.X,
                     op=mybir.AluOpType.max,
                 )
+
+        def first_convolution(r_in):
             for r_out in range(SLOTS):
                 nc.tensor.matmul(
                     h_sum(r_out),
@@ -119,11 +131,23 @@ def tile_c3dnet_kernel(tc, x, dt_w, dt_gain, dt_bias, d4_w, d4_gain, d4_bias, of
                     stop=(r_in == SLOTS - 1 and r_out % PER_BANK == PER_BANK - 1),
                 )
 
-        for r_in in range(SLOTS):
+        def pooled_share(r_in):
             for q_out in range(OUT_SLOTS):
                 nc.tensor.matmul(
                     out_sums[q_out][:], d4_pooled_weights(r_in, q_out), pooled[r_in][:], start=(r_in == 0), stop=False
                 )
+
+        for r in range(SLOTS):
+            pool(r)
+        for r_in in range(D4_POOLED_PIECE):
+            first_convolution(r_in)
+        for r_in in range(D4_POOLED_PIECE):
+            pooled_share(r_in)
+        for r_in in range(D4_POOLED_PIECE, SLOTS):
+            first_convolution(r_in)
+        for r_in in range(D4_POOLED_PIECE, SLOTS):
+            pooled_share(r_in)
+
         h = [held.tile([P, SAMPLED], BF16, name=f"h{r}") for r in range(SLOTS)]
         for r in range(SLOTS):
             nc.scalar.activation(h[r][:], h_sum(r), RELU, bias=dt_biases[:, r : r + 1], scale=dt_gains[:, r : r + 1])
@@ -137,7 +161,7 @@ def tile_c3dnet_kernel(tc, x, dt_w, dt_gain, dt_bias, d4_w, d4_gain, d4_bias, of
         result = held.tile([P, OUT_SLOTS, SAMPLED], F32, name="result")
         for q in range(OUT_SLOTS):
             gain, bias = d4_gains[:, q : q + 1], d4_biases[:, q : q + 1]
-            if q % 2 == 0:
+            if q % 2 == 1:
                 nc.scalar.activation(result[:, q, :], out_sums[q][:], RELU, bias=bias, scale=gain)
             else:
                 nc.vector.tensor_scalar(

@@ -20,7 +20,8 @@ PER_BANK = BANK // SAMPLED
 X_PIECE = 2
 DT_PIECE = 2
 D4_POOLED_PIECE = 4
-D4_H_PIECE = 4
+D4_H_PIECES = (4, 2, 1, 1)
+D4_H_FIRST = tuple(sum(D4_H_PIECES[:k]) for k in range(len(D4_H_PIECES)))
 
 FLOPS = 2 * SAMPLED * (CHANNELS * CHANNELS + 2 * CHANNELS * OUT_CHANNELS)
 
@@ -46,7 +47,7 @@ def tile_c3dnet_kernel(tc, x, dt_w, dt_gain, dt_bias, d4_w, d4_gain, d4_bias, of
             for k in range(SLOTS // D4_POOLED_PIECE)
         ]
         d4_h_pieces = [
-            held.tile([P, D4_H_PIECE, OUT_CHANNELS], BF16, name=f"d4_h{k}") for k in range(SLOTS // D4_H_PIECE)
+            held.tile([P, slots, OUT_CHANNELS], BF16, name=f"d4_h{k}") for k, slots in enumerate(D4_H_PIECES)
         ]
 
         def load_x(k):
@@ -61,7 +62,7 @@ def tile_c3dnet_kernel(tc, x, dt_w, dt_gain, dt_bias, d4_w, d4_gain, d4_bias, of
             )
 
         def load_d4_h(k):
-            nc.sync.dma_start(d4_h_pieces[k][:], d4_h_by_slot[:, k * D4_H_PIECE : (k + 1) * D4_H_PIECE, :])
+            nc.sync.dma_start(d4_h_pieces[k][:], d4_h_by_slot[:, D4_H_FIRST[k] : D4_H_FIRST[k] + D4_H_PIECES[k], :])
 
         load_x(0)
         nc.sync.dma_start(offsets[:], offs)
@@ -74,8 +75,8 @@ def tile_c3dnet_kernel(tc, x, dt_w, dt_gain, dt_bias, d4_w, d4_gain, d4_bias, of
         load_dt(2)
         load_dt(3)
         load_d4_pooled(1)
-        load_d4_h(0)
-        load_d4_h(1)
+        for k in range(len(D4_H_PIECES)):
+            load_d4_h(k)
 
         def every_nth_column(rows, step, first):
             return rows.rearrange("p (m r) -> p r m", r=step)[:, first, :]
@@ -86,9 +87,6 @@ def tile_c3dnet_kernel(tc, x, dt_w, dt_gain, dt_bias, d4_w, d4_gain, d4_bias, of
         def d4_pooled_weights(r_in, q_out):
             rows = d4_pooled_pieces[r_in // D4_POOLED_PIECE][:, r_in % D4_POOLED_PIECE, :]
             return every_nth_column(rows, OUT_SLOTS, q_out)
-
-        def d4_h_weights(r_in, q_out):
-            return every_nth_column(d4_h_pieces[r_in // D4_H_PIECE][:, r_in % D4_H_PIECE, :], OUT_SLOTS, q_out)
 
         dt_gains = held.tile([P, SLOTS], F32, name="dt_gains")
         dt_biases = held.tile([P, SLOTS], F32, name="dt_biases")
@@ -151,11 +149,16 @@ def tile_c3dnet_kernel(tc, x, dt_w, dt_gain, dt_bias, d4_w, d4_gain, d4_bias, of
         h = [held.tile([P, SAMPLED], BF16, name=f"h{r}") for r in range(SLOTS)]
         for r in range(SLOTS):
             nc.scalar.activation(h[r][:], h_sum(r), RELU, bias=dt_biases[:, r : r + 1], scale=dt_gains[:, r : r + 1])
-        for k in range(SLOTS // D4_H_PIECE):
+        for k, slots in enumerate(D4_H_PIECES):
             for q_out in range(OUT_SLOTS):
-                for r_in in range(k * D4_H_PIECE, (k + 1) * D4_H_PIECE):
+                for j in range(slots):
+                    r_in = D4_H_FIRST[k] + j
                     nc.tensor.matmul(
-                        out_sums[q_out][:], d4_h_weights(r_in, q_out), h[r_in][:], start=False, stop=(r_in == SLOTS - 1)
+                        out_sums[q_out][:],
+                        every_nth_column(d4_h_pieces[k][:, j, :], OUT_SLOTS, q_out),
+                        h[r_in][:],
+                        start=False,
+                        stop=(r_in == SLOTS - 1),
                     )
         out_by_slot = out.rearrange("(p q) n -> p q n", q=OUT_SLOTS)
         result = held.tile([P, OUT_SLOTS, SAMPLED], F32, name="result")

@@ -50,6 +50,14 @@ def tile_c3dnet_kernel(tc, x, dt_w, dt_gain, dt_bias, d4_w, d4_gain, d4_bias, of
             held.tile([P, slots, OUT_CHANNELS], BF16, name=f"d4_h{k}") for k, slots in enumerate(D4_H_PIECES)
         ]
 
+        dt_gains = held.tile([P, SLOTS], F32, name="dt_gains")
+        dt_biases = held.tile([P, SLOTS], F32, name="dt_biases")
+        d4_gains = held.tile([P, OUT_SLOTS], F32, name="d4_gains")
+        d4_biases = held.tile([P, OUT_SLOTS], F32, name="d4_biases")
+
+        def load_columns(columns, vector):
+            nc.sync.dma_start(columns[:], vector.rearrange("(p r) one -> p (r one)", p=P))
+
         def load_x(k):
             nc.sync.dma_start(x_pieces[k][:], x_by_slot[:, k * X_PIECE : (k + 1) * X_PIECE, :])
 
@@ -72,11 +80,15 @@ def tile_c3dnet_kernel(tc, x, dt_w, dt_gain, dt_bias, d4_w, d4_gain, d4_bias, of
         load_dt(1)
         load_d4_pooled(0)
         load_x(3)
+        load_columns(dt_gains, dt_gain)
+        load_columns(dt_biases, dt_bias)
         load_dt(2)
         load_dt(3)
         load_d4_pooled(1)
         for k in range(len(D4_H_PIECES)):
             load_d4_h(k)
+        load_columns(d4_gains, d4_gain)
+        load_columns(d4_biases, d4_bias)
 
         def every_nth_column(rows, step, first):
             return rows.rearrange("p (m r) -> p r m", r=step)[:, first, :]
@@ -87,13 +99,6 @@ def tile_c3dnet_kernel(tc, x, dt_w, dt_gain, dt_bias, d4_w, d4_gain, d4_bias, of
         def d4_pooled_weights(r_in, q_out):
             rows = d4_pooled_pieces[r_in // D4_POOLED_PIECE][:, r_in % D4_POOLED_PIECE, :]
             return every_nth_column(rows, OUT_SLOTS, q_out)
-
-        dt_gains = held.tile([P, SLOTS], F32, name="dt_gains")
-        dt_biases = held.tile([P, SLOTS], F32, name="dt_biases")
-        d4_gains = held.tile([P, OUT_SLOTS], F32, name="d4_gains")
-        d4_biases = held.tile([P, OUT_SLOTS], F32, name="d4_biases")
-        for columns, vector in ((dt_gains, dt_gain), (dt_biases, dt_bias), (d4_gains, d4_gain), (d4_biases, d4_bias)):
-            nc.gpsimd.dma_start(columns[:], vector.rearrange("(p r) one -> p (r one)", p=P))
 
         zeros = held.tile([P, BANK], BF16, name="zeros")
         nc.scalar.memzero(zeros[:])

@@ -17,7 +17,8 @@ SLOTS = CHANNELS // P
 OUT_SLOTS = OUT_CHANNELS // P
 BANK = 512
 PER_BANK = BANK // SAMPLED
-X_PIECE = 2
+X_PIECES = (2, 2, 2, 1, 1)
+X_FIRST = tuple(sum(X_PIECES[:k]) for k in range(len(X_PIECES)))
 DT_PIECE = 2
 D4_POOLED_PIECE = 4
 D4_H_PIECES = (4, 2, 1, 1)
@@ -40,7 +41,8 @@ def tile_c3dnet_kernel(tc, x, dt_w, dt_gain, dt_bias, d4_w, d4_gain, d4_bias, of
         d4_h_by_slot = d4_w[0:CHANNELS, :].rearrange("(p r) o -> p r o", r=SLOTS)
         d4_pooled_by_slot = d4_w[CHANNELS : 2 * CHANNELS, :].rearrange("(p r) o -> p r o", r=SLOTS)
 
-        x_pieces = [held.tile([P, X_PIECE, POINTS], F32, name=f"x{k}") for k in range(SLOTS // X_PIECE)]
+        x_pieces = [held.tile([P, slots, POINTS], F32, name=f"x{k}") for k, slots in enumerate(X_PIECES)]
+        x_windows = [x_pieces[k][:, j, :] for k, slots in enumerate(X_PIECES) for j in range(slots)]
         dt_pieces = [held.tile([P, DT_PIECE, CHANNELS], BF16, name=f"dt{k}") for k in range(SLOTS // DT_PIECE)]
         d4_pooled_pieces = [
             held.tile([P, D4_POOLED_PIECE, OUT_CHANNELS], BF16, name=f"d4_pooled{k}")
@@ -59,7 +61,7 @@ def tile_c3dnet_kernel(tc, x, dt_w, dt_gain, dt_bias, d4_w, d4_gain, d4_bias, of
             nc.sync.dma_start(columns[:], vector.rearrange("(p r) one -> p (r one)", p=P))
 
         def load_x(k):
-            nc.sync.dma_start(x_pieces[k][:], x_by_slot[:, k * X_PIECE : (k + 1) * X_PIECE, :])
+            nc.sync.dma_start(x_pieces[k][:], x_by_slot[:, X_FIRST[k] : X_FIRST[k] + X_PIECES[k], :])
 
         def load_dt(k):
             nc.sync.dma_start(dt_pieces[k][:], dt_by_slot[:, k * DT_PIECE : (k + 1) * DT_PIECE, :])
@@ -77,9 +79,10 @@ def tile_c3dnet_kernel(tc, x, dt_w, dt_gain, dt_bias, d4_w, d4_gain, d4_bias, of
         load_x(1)
         load_x(2)
         load_dt(0)
-        load_dt(1)
-        load_d4_pooled(0)
         load_x(3)
+        load_dt(1)
+        load_x(4)
+        load_d4_pooled(0)
         load_columns(dt_gains, dt_gain)
         load_columns(dt_biases, dt_bias)
         load_dt(2)
@@ -115,7 +118,7 @@ def tile_c3dnet_kernel(tc, x, dt_w, dt_gain, dt_bias, d4_w, d4_gain, d4_bias, of
 
         def pool(r):
             picked = ring.tile([P, LISTED], F32, name="picked")
-            nc.scalar.activation(picked[:], x_pieces[r // X_PIECE][:, r % X_PIECE, :].indirect(offsets[:]), COPY)
+            nc.scalar.activation(picked[:], x_windows[r].indirect(offsets[:]), COPY)
             with nc.allow_low_precision(reason="a maximum is one of its inputs: the only rounding is the asked one to bfloat16"):
                 nc.vector.tensor_reduce(
                     pooled[r][:],

@@ -17,9 +17,10 @@ SLOTS = CHANNELS // P
 OUT_SLOTS = OUT_CHANNELS // P
 BANK = 512
 PER_BANK = BANK // SAMPLED
-X_PIECES = (2, 2, 2, 1, 1)
+X_PIECES = (4, 2, 1, 1)
 X_FIRST = tuple(sum(X_PIECES[:k]) for k in range(len(X_PIECES)))
-DT_PIECE = 2
+DT_PIECES = (4, 2, 2)
+DT_FIRST = tuple(sum(DT_PIECES[:k]) for k in range(len(DT_PIECES)))
 D4_POOLED_PIECE = 4
 D4_H_PIECES = (4, 2, 1, 1)
 D4_H_FIRST = tuple(sum(D4_H_PIECES[:k]) for k in range(len(D4_H_PIECES)))
@@ -43,7 +44,8 @@ def tile_c3dnet_kernel(tc, x, dt_w, dt_gain, dt_bias, d4_w, d4_gain, d4_bias, of
 
         x_pieces = [held.tile([P, slots, POINTS], F32, name=f"x{k}") for k, slots in enumerate(X_PIECES)]
         x_windows = [x_pieces[k][:, j, :] for k, slots in enumerate(X_PIECES) for j in range(slots)]
-        dt_pieces = [held.tile([P, DT_PIECE, CHANNELS], BF16, name=f"dt{k}") for k in range(SLOTS // DT_PIECE)]
+        dt_pieces = [held.tile([P, slots, CHANNELS], BF16, name=f"dt{k}") for k, slots in enumerate(DT_PIECES)]
+        dt_rows = [dt_pieces[k][:, j, :] for k, slots in enumerate(DT_PIECES) for j in range(slots)]
         d4_pooled_pieces = [
             held.tile([P, D4_POOLED_PIECE, OUT_CHANNELS], BF16, name=f"d4_pooled{k}")
             for k in range(SLOTS // D4_POOLED_PIECE)
@@ -64,7 +66,7 @@ def tile_c3dnet_kernel(tc, x, dt_w, dt_gain, dt_bias, d4_w, d4_gain, d4_bias, of
             nc.sync.dma_start(x_pieces[k][:], x_by_slot[:, X_FIRST[k] : X_FIRST[k] + X_PIECES[k], :])
 
         def load_dt(k):
-            nc.sync.dma_start(dt_pieces[k][:], dt_by_slot[:, k * DT_PIECE : (k + 1) * DT_PIECE, :])
+            nc.sync.dma_start(dt_pieces[k][:], dt_by_slot[:, DT_FIRST[k] : DT_FIRST[k] + DT_PIECES[k], :])
 
         def load_d4_pooled(k):
             nc.sync.dma_start(
@@ -77,16 +79,14 @@ def tile_c3dnet_kernel(tc, x, dt_w, dt_gain, dt_bias, d4_w, d4_gain, d4_bias, of
         load_x(0)
         nc.sync.dma_start(offsets[:], offs)
         load_x(1)
-        load_x(2)
         load_dt(0)
-        load_x(3)
-        load_dt(1)
-        load_x(4)
+        load_x(2)
         load_d4_pooled(0)
+        load_x(3)
         load_columns(dt_gains, dt_gain)
         load_columns(dt_biases, dt_bias)
+        load_dt(1)
         load_dt(2)
-        load_dt(3)
         load_d4_pooled(1)
         for k in range(len(D4_H_PIECES)):
             load_d4_h(k)
@@ -97,7 +97,7 @@ def tile_c3dnet_kernel(tc, x, dt_w, dt_gain, dt_bias, d4_w, d4_gain, d4_bias, of
             return rows.rearrange("p (m r) -> p r m", r=step)[:, first, :]
 
         def dt_weights(r_in, r_out):
-            return every_nth_column(dt_pieces[r_in // DT_PIECE][:, r_in % DT_PIECE, :], SLOTS, r_out)
+            return every_nth_column(dt_rows[r_in], SLOTS, r_out)
 
         def d4_pooled_weights(r_in, q_out):
             rows = d4_pooled_pieces[r_in // D4_POOLED_PIECE][:, r_in % D4_POOLED_PIECE, :]

@@ -1,4 +1,5 @@
 import concourse.mybir as mybir
+from concourse.masks import make_identity
 
 F32 = mybir.dt.float32
 BF16 = mybir.dt.bfloat16
@@ -15,6 +16,7 @@ SAMPLED = LISTED // NEIGHBOURS
 OUT_CHANNELS = 512
 SLOTS = CHANNELS // P
 OUT_SLOTS = OUT_CHANNELS // P
+VECTOR_ROWS = 64
 BANK = 512
 PER_BANK = BANK // SAMPLED
 X_PIECES = (4, 2, 1, 1)
@@ -39,7 +41,7 @@ def tile_c3dnet_kernel(tc, x, dt_w, dt_gain, dt_bias, d4_w, d4_gain, d4_bias, of
 
         x_by_slot = x.rearrange("(p r) s -> p r s", r=SLOTS)
         dt_by_slot = dt_w.rearrange("(p r) m -> p r m", r=SLOTS)
-        d4_h_by_slot = d4_w[0:CHANNELS, :].rearrange("(p r) o -> p r o", r=SLOTS)
+        d4_h_by_slot = d4_w[0:CHANNELS, :].rearrange("(r p) o -> p r o", p=P)
         d4_pooled_by_slot = d4_w[CHANNELS : 2 * CHANNELS, :].rearrange("(p r) o -> p r o", r=SLOTS)
 
         x_pieces = [held.tile([P, slots, POINTS], F32, name=f"x{k}") for k, slots in enumerate(X_PIECES)]
@@ -54,13 +56,15 @@ def tile_c3dnet_kernel(tc, x, dt_w, dt_gain, dt_bias, d4_w, d4_gain, d4_bias, of
             held.tile([P, slots, OUT_CHANNELS], BF16, name=f"d4_h{k}") for k, slots in enumerate(D4_H_PIECES)
         ]
 
-        dt_gains = held.tile([P, SLOTS], F32, name="dt_gains")
-        dt_biases = held.tile([P, SLOTS], F32, name="dt_biases")
-        d4_gains = held.tile([P, OUT_SLOTS], F32, name="d4_gains")
-        d4_biases = held.tile([P, OUT_SLOTS], F32, name="d4_biases")
+        vector_rows = held.tile([VECTOR_ROWS, P], F32, name="vector_rows")
+        nc.vector.memset(vector_rows[:], 0.0)
+        vectors = (dt_gain, dt_bias, d4_gain, d4_bias)
+        vector_slots = (SLOTS, SLOTS, OUT_SLOTS, OUT_SLOTS)
+        vector_first = [sum(vector_slots[:k]) for k in range(len(vectors))]
 
-        def load_columns(columns, vector):
-            nc.sync.dma_start(columns[:], vector.rearrange("(p r) one -> p (r one)", p=P))
+        def load_vector(k):
+            rows = vector_rows[vector_first[k] : vector_first[k] + vector_slots[k], :]
+            nc.sync.dma_start(rows, vectors[k].rearrange("(r p) one -> r (p one)", p=P))
 
         def load_x(k):
             nc.sync.dma_start(x_pieces[k][:], x_by_slot[:, X_FIRST[k] : X_FIRST[k] + X_PIECES[k], :])
@@ -78,30 +82,38 @@ def tile_c3dnet_kernel(tc, x, dt_w, dt_gain, dt_bias, d4_w, d4_gain, d4_bias, of
 
         load_x(0)
         nc.sync.dma_start(offsets[:], offs)
+        for k in range(len(vectors)):
+            load_vector(k)
         load_x(1)
         load_dt(0)
         load_x(2)
         load_d4_pooled(0)
         load_x(3)
-        load_columns(dt_gains, dt_gain)
-        load_columns(dt_biases, dt_bias)
         load_dt(1)
         load_dt(2)
         load_d4_pooled(1)
         for k in range(len(D4_H_PIECES)):
             load_d4_h(k)
-        load_columns(d4_gains, d4_gain)
-        load_columns(d4_biases, d4_bias)
 
-        def every_nth_column(rows, step, first):
-            return rows.rearrange("p (m r) -> p r m", r=step)[:, first, :]
+        def block(rows, k):
+            return rows[:, k * P : (k + 1) * P]
 
         def dt_weights(r_in, r_out):
-            return every_nth_column(dt_rows[r_in], SLOTS, r_out)
+            return block(dt_rows[r_in], r_out)
 
         def d4_pooled_weights(r_in, q_out):
             rows = d4_pooled_pieces[r_in // D4_POOLED_PIECE][:, r_in % D4_POOLED_PIECE, :]
-            return every_nth_column(rows, OUT_SLOTS, q_out)
+            return block(rows, q_out)
+
+        identity = held.tile([VECTOR_ROWS, VECTOR_ROWS], F32, name="identity")
+        make_identity(nc, identity[:])
+        flipped = psum.tile([P, VECTOR_ROWS], F32, name="flipped")
+        nc.tensor.transpose(flipped[:], vector_rows[:], identity[:])
+        vector_columns = held.tile([P, sum(vector_slots)], F32, name="vector_columns")
+        nc.vector.tensor_copy(vector_columns[:], flipped[:, 0 : sum(vector_slots)])
+        dt_gains, dt_biases, d4_gains, d4_biases = [
+            vector_columns[:, first : first + slots] for first, slots in zip(vector_first, vector_slots)
+        ]
 
         zeros = held.tile([P, BANK], BF16, name="zeros")
         nc.scalar.memzero(zeros[:])
@@ -163,12 +175,12 @@ def tile_c3dnet_kernel(tc, x, dt_w, dt_gain, dt_bias, d4_w, d4_gain, d4_bias, of
                     r_in = D4_H_FIRST[k] + j
                     nc.tensor.matmul(
                         out_sums[q_out][:],
-                        every_nth_column(d4_h_pieces[k][:, j, :], OUT_SLOTS, q_out),
+                        block(d4_h_pieces[k][:, j, :], q_out),
                         h[r_in][:],
                         start=False,
                         stop=(r_in == SLOTS - 1),
                     )
-        out_by_slot = out.rearrange("(p q) n -> p q n", q=OUT_SLOTS)
+        out_by_slot = out.rearrange("(q p) n -> p q n", p=P)
         result = held.tile([P, OUT_SLOTS, SAMPLED], F32, name="result")
         for q in range(OUT_SLOTS):
             gain, bias = d4_gains[:, q : q + 1], d4_biases[:, q : q + 1]

@@ -24,8 +24,8 @@ X_FIRST = tuple(sum(X_PIECES[:k]) for k in range(len(X_PIECES)))
 DT_PIECES = (4, 2, 2)
 DT_FIRST = tuple(sum(DT_PIECES[:k]) for k in range(len(DT_PIECES)))
 D4_POOLED_PIECE = 4
-D4_H_PIECES = (4, 2, 1, 1)
-D4_H_FIRST = tuple(sum(D4_H_PIECES[:k]) for k in range(len(D4_H_PIECES)))
+OUT_HALF = OUT_SLOTS // 2
+D4_H_PIECES = ((0, 4, 0, OUT_SLOTS), (4, 2, 0, OUT_SLOTS), (6, 2, 0, OUT_HALF), (6, 2, OUT_HALF, OUT_HALF))
 
 FLOPS = 2 * SAMPLED * (CHANNELS * CHANNELS + 2 * CHANNELS * OUT_CHANNELS)
 
@@ -53,7 +53,8 @@ def tile_c3dnet_kernel(tc, x, dt_w, dt_gain, dt_bias, d4_w, d4_gain, d4_bias, of
             for k in range(SLOTS // D4_POOLED_PIECE)
         ]
         d4_h_pieces = [
-            held.tile([P, slots, OUT_CHANNELS], BF16, name=f"d4_h{k}") for k, slots in enumerate(D4_H_PIECES)
+            held.tile([P, slots, out_slots * P], BF16, name=f"d4_h{k}")
+            for k, (first, slots, out_first, out_slots) in enumerate(D4_H_PIECES)
         ]
 
         vector_rows = held.tile([VECTOR_ROWS, P], F32, name="vector_rows")
@@ -78,7 +79,11 @@ def tile_c3dnet_kernel(tc, x, dt_w, dt_gain, dt_bias, d4_w, d4_gain, d4_bias, of
             )
 
         def load_d4_h(k):
-            nc.sync.dma_start(d4_h_pieces[k][:], d4_h_by_slot[:, D4_H_FIRST[k] : D4_H_FIRST[k] + D4_H_PIECES[k], :])
+            first, slots, out_first, out_slots = D4_H_PIECES[k]
+            nc.sync.dma_start(
+                d4_h_pieces[k][:],
+                d4_h_by_slot[:, first : first + slots, out_first * P : (out_first + out_slots) * P],
+            )
 
         load_x(0)
         nc.sync.dma_start(offsets[:], offs)
@@ -169,20 +174,10 @@ def tile_c3dnet_kernel(tc, x, dt_w, dt_gain, dt_bias, d4_w, d4_gain, d4_bias, of
         h = [held.tile([P, SAMPLED], BF16, name=f"h{r}") for r in range(SLOTS)]
         for r in range(SLOTS):
             nc.scalar.activation(h[r][:], h_sum(r), RELU, bias=dt_biases[:, r : r + 1], scale=dt_gains[:, r : r + 1])
-        for k, slots in enumerate(D4_H_PIECES):
-            for q_out in range(OUT_SLOTS):
-                for j in range(slots):
-                    r_in = D4_H_FIRST[k] + j
-                    nc.tensor.matmul(
-                        out_sums[q_out][:],
-                        block(d4_h_pieces[k][:, j, :], q_out),
-                        h[r_in][:],
-                        start=False,
-                        stop=(r_in == SLOTS - 1),
-                    )
         out_by_slot = out.rearrange("(q p) n -> p q n", p=P)
         result = held.tile([P, OUT_SLOTS, SAMPLED], F32, name="result")
-        for q in range(OUT_SLOTS):
+
+        def finish(q):
             gain, bias = d4_gains[:, q : q + 1], d4_biases[:, q : q + 1]
             if q % 2 == 1:
                 nc.scalar.activation(result[:, q, :], out_sums[q][:], RELU, bias=bias, scale=gain)
@@ -192,3 +187,16 @@ def tile_c3dnet_kernel(tc, x, dt_w, dt_gain, dt_bias, d4_w, d4_gain, d4_bias, of
                 )
                 nc.vector.tensor_scalar_max(result[:, q, :], result[:, q, :], 0.0)
             nc.sync.dma_start(out_by_slot[:, q, :], result[:, q, :])
+
+        for k, (first, slots, out_first, out_slots) in enumerate(D4_H_PIECES):
+            for q_out in range(out_first, out_first + out_slots):
+                for r_in in range(first, first + slots):
+                    nc.tensor.matmul(
+                        out_sums[q_out][:],
+                        block(d4_h_pieces[k][:, r_in - first, :], q_out - out_first),
+                        h[r_in][:],
+                        start=False,
+                        stop=(r_in == SLOTS - 1),
+                    )
+                if first + slots == SLOTS:
+                    finish(q_out)

@@ -67,8 +67,8 @@ def tile_c3dnet_kernel(tc, x, dt_w, dt_gain, dt_bias, d4_w, d4_gain, d4_bias, of
             rows = vector_rows[vector_first[k] : vector_first[k] + vector_slots[k], :]
             nc.sync.dma_start(rows, vectors[k].rearrange("(r p) one -> r (p one)", p=P))
 
-        def load_x(k):
-            nc.sync.dma_start(x_pieces[k][:], x_by_slot[:, X_FIRST[k] : X_FIRST[k] + X_PIECES[k], :])
+        def load_x(queue, k):
+            queue.dma_start(x_pieces[k][:], x_by_slot[:, X_FIRST[k] : X_FIRST[k] + X_PIECES[k], :])
 
         def load_dt(k):
             nc.sync.dma_start(dt_pieces[k][:], dt_by_slot[:, DT_FIRST[k] : DT_FIRST[k] + DT_PIECES[k], :])
@@ -85,15 +85,15 @@ def tile_c3dnet_kernel(tc, x, dt_w, dt_gain, dt_bias, d4_w, d4_gain, d4_bias, of
                 d4_h_by_slot[:, first : first + slots, out_first * P : (out_first + out_slots) * P],
             )
 
-        load_x(0)
+        load_x(nc.scalar, 0)
         nc.sync.dma_start(offsets[:], offs)
         for k in range(len(vectors)):
             load_vector(k)
-        load_x(1)
+        load_x(nc.sync, 1)
         load_dt(0)
-        load_x(2)
+        load_x(nc.sync, 2)
         load_d4_pooled(0)
-        load_x(3)
+        load_x(nc.sync, 3)
         load_dt(1)
         load_dt(2)
         load_d4_pooled(1)
@@ -181,12 +181,14 @@ def tile_c3dnet_kernel(tc, x, dt_w, dt_gain, dt_bias, d4_w, d4_gain, d4_bias, of
             gain, bias = d4_gains[:, q : q + 1], d4_biases[:, q : q + 1]
             if q % 2 == 1:
                 nc.scalar.activation(result[:, q, :], out_sums[q][:], RELU, bias=bias, scale=gain)
+                queue = nc.scalar
             else:
                 nc.vector.tensor_scalar(
                     result[:, q, :], out_sums[q][:], gain, bias, op0=mybir.AluOpType.mult, op1=mybir.AluOpType.add
                 )
                 nc.vector.tensor_scalar_max(result[:, q, :], result[:, q, :], 0.0)
-            nc.sync.dma_start(out_by_slot[:, q, :], result[:, q, :])
+                queue = nc.sync
+            queue.dma_start(out_by_slot[:, q, :], result[:, q, :])
 
         for k, (first, slots, out_first, out_slots) in enumerate(D4_H_PIECES):
             for q_out in range(out_first, out_first + out_slots):

@@ -67,8 +67,8 @@ def tile_c3dnet_kernel(tc, x, dt_w, dt_gain, dt_bias, d4_w, d4_gain, d4_bias, of
             rows = vector_rows[vector_first[k] : vector_first[k] + vector_slots[k], :]
             nc.sync.dma_start(rows, vectors[k].rearrange("(r p) one -> r (p one)", p=P))
 
-        def load_x(queue, k):
-            queue.dma_start(x_pieces[k][:], x_by_slot[:, X_FIRST[k] : X_FIRST[k] + X_PIECES[k], :])
+        def load_x(k):
+            nc.sync.dma_start(x_pieces[k][:], x_by_slot[:, X_FIRST[k] : X_FIRST[k] + X_PIECES[k], :])
 
         def load_dt(k):
             nc.sync.dma_start(dt_pieces[k][:], dt_by_slot[:, DT_FIRST[k] : DT_FIRST[k] + DT_PIECES[k], :])
@@ -85,15 +85,15 @@ def tile_c3dnet_kernel(tc, x, dt_w, dt_gain, dt_bias, d4_w, d4_gain, d4_bias, of
                 d4_h_by_slot[:, first : first + slots, out_first * P : (out_first + out_slots) * P],
             )
 
-        load_x(nc.scalar, 0)
+        load_x(0)
         nc.sync.dma_start(offsets[:], offs)
         for k in range(len(vectors)):
             load_vector(k)
-        load_x(nc.sync, 1)
+        load_x(1)
         load_dt(0)
-        load_x(nc.sync, 2)
+        load_x(2)
         load_d4_pooled(0)
-        load_x(nc.sync, 3)
+        load_x(3)
         load_dt(1)
         load_dt(2)
         load_d4_pooled(1)

@@ -19,9 +19,9 @@ OUT_SLOTS = OUT_CHANNELS // P
 VECTOR_ROWS = 64
 BANK = 512
 PER_BANK = BANK // SAMPLED
-X_PIECES = (4, 2, 1, 1)
+X_PIECES = (2, 2, 2, 1, 1)
 X_FIRST = tuple(sum(X_PIECES[:k]) for k in range(len(X_PIECES)))
-DT_PIECES = (4, 2, 2)
+DT_PIECES = (4, 1, 1, 2)
 DT_FIRST = tuple(sum(DT_PIECES[:k]) for k in range(len(DT_PIECES)))
 D4_POOLED_PIECE = 4
 OUT_HALF = OUT_SLOTS // 2
@@ -90,12 +90,13 @@ def tile_c3dnet_kernel(tc, x, dt_w, dt_gain, dt_bias, d4_w, d4_gain, d4_bias, of
         for k in range(len(vectors)):
             load_vector(k)
         load_x(1)
-        load_dt(0)
         load_x(2)
-        load_d4_pooled(0)
+        load_dt(0)
         load_x(3)
-        load_dt(1)
-        load_dt(2)
+        load_d4_pooled(0)
+        load_x(4)
+        for k in range(1, len(DT_PIECES)):
+            load_dt(k)
         load_d4_pooled(1)
         for k in range(len(D4_H_PIECES)):
             load_d4_h(k)
@@ -179,15 +180,8 @@ def tile_c3dnet_kernel(tc, x, dt_w, dt_gain, dt_bias, d4_w, d4_gain, d4_bias, of
 
         def finish(q):
             gain, bias = d4_gains[:, q : q + 1], d4_biases[:, q : q + 1]
-            if q % 2 == 1:
-                nc.scalar.activation(result[:, q, :], out_sums[q][:], RELU, bias=bias, scale=gain)
-                queue = nc.scalar
-            else:
-                nc.vector.tensor_scalar(
-                    result[:, q, :], out_sums[q][:], gain, bias, op0=mybir.AluOpType.mult, op1=mybir.AluOpType.add
-                )
-                nc.vector.tensor_scalar_max(result[:, q, :], result[:, q, :], 0.0)
-                queue = nc.sync
+            nc.scalar.activation(result[:, q, :], out_sums[q][:], RELU, bias=bias, scale=gain)
+            queue = nc.sync if q % 2 == 0 else nc.scalar
             queue.dma_start(out_by_slot[:, q, :], result[:, q, :])
 
         for k, (first, slots, out_first, out_slots) in enumerate(D4_H_PIECES):

@@ -17,6 +17,7 @@ OUT_CHANNELS = 512
 SLOTS = CHANNELS // P
 OUT_SLOTS = OUT_CHANNELS // P
 VECTOR_ROWS = 64
+DMA_STEP = 256
 BANK = 512
 PER_BANK = BANK // SAMPLED
 X_PIECES = (2, 2, 2, 1, 1)
@@ -44,20 +45,20 @@ def tile_c3dnet_kernel(tc, x, dt_w, dt_gain, dt_bias, d4_w, d4_gain, d4_bias, of
         d4_h_by_slot = d4_w[0:CHANNELS, :].rearrange("(r p) o -> p r o", p=P)
         d4_pooled_by_slot = d4_w[CHANNELS : 2 * CHANNELS, :].rearrange("(p r) o -> p r o", r=SLOTS)
 
-        x_pieces = [held.tile([P, slots, POINTS], F32, name=f"x{k}") for k, slots in enumerate(X_PIECES)]
+        x_pieces = [held.tile([P, slots, POINTS], F32, name=f"x{k}", align_bytes=DMA_STEP) for k, slots in enumerate(X_PIECES)]
         x_windows = [x_pieces[k][:, j, :] for k, slots in enumerate(X_PIECES) for j in range(slots)]
-        dt_pieces = [held.tile([P, slots, CHANNELS], BF16, name=f"dt{k}") for k, slots in enumerate(DT_PIECES)]
+        dt_pieces = [held.tile([P, slots, CHANNELS], BF16, name=f"dt{k}", align_bytes=DMA_STEP) for k, slots in enumerate(DT_PIECES)]
         dt_rows = [dt_pieces[k][:, j, :] for k, slots in enumerate(DT_PIECES) for j in range(slots)]
         d4_pooled_pieces = [
-            held.tile([P, D4_POOLED_PIECE, OUT_CHANNELS], BF16, name=f"d4_pooled{k}")
+            held.tile([P, D4_POOLED_PIECE, OUT_CHANNELS], BF16, name=f"d4_pooled{k}", align_bytes=DMA_STEP)
             for k in range(SLOTS // D4_POOLED_PIECE)
         ]
         d4_h_pieces = [
-            held.tile([P, slots, out_slots * P], BF16, name=f"d4_h{k}")
+            held.tile([P, slots, out_slots * P], BF16, name=f"d4_h{k}", align_bytes=DMA_STEP)
             for k, (first, slots, out_first, out_slots) in enumerate(D4_H_PIECES)
         ]
 
-        vector_rows = held.tile([VECTOR_ROWS, P], F32, name="vector_rows")
+        vector_rows = held.tile([VECTOR_ROWS, P], F32, name="vector_rows", align_bytes=DMA_STEP)
         nc.vector.memset(vector_rows[:], 0.0)
         vectors = (dt_gain, dt_bias, d4_gain, d4_bias)
         vector_slots = (SLOTS, SLOTS, OUT_SLOTS, OUT_SLOTS)
@@ -176,7 +177,7 @@ def tile_c3dnet_kernel(tc, x, dt_w, dt_gain, dt_bias, d4_w, d4_gain, d4_bias, of
         for r in range(SLOTS):
             nc.scalar.activation(h[r][:], h_sum(r), RELU, bias=dt_biases[:, r : r + 1], scale=dt_gains[:, r : r + 1])
         out_by_slot = out.rearrange("(q p) n -> p q n", p=P)
-        result = held.tile([P, OUT_SLOTS, SAMPLED], F32, name="result")
+        result = held.tile([P, OUT_SLOTS, SAMPLED], F32, name="result", align_bytes=DMA_STEP)
 
         def finish(q):
             gain, bias = d4_gains[:, q : q + 1], d4_biases[:, q : q + 1]

@@ -20,9 +20,9 @@ VECTOR_ROWS = 64
 DMA_STEP = 256
 BANK = 512
 PER_BANK = BANK // SAMPLED
-X_PIECES = (2, 2, 2, 1, 1)
+X_PIECES = (2, 4, 1, 1)
 X_FIRST = tuple(sum(X_PIECES[:k]) for k in range(len(X_PIECES)))
-DT_PIECES = (4, 1, 1, 2)
+DT_PIECES = (4, 2, 2)
 DT_FIRST = tuple(sum(DT_PIECES[:k]) for k in range(len(DT_PIECES)))
 D4_POOLED_PIECE = 4
 OUT_HALF = OUT_SLOTS // 2
@@ -91,11 +91,10 @@ def tile_c3dnet_kernel(tc, x, dt_w, dt_gain, dt_bias, d4_w, d4_gain, d4_bias, of
         for k in range(len(vectors)):
             load_vector(k)
         load_x(1)
-        load_x(2)
         load_dt(0)
-        load_x(3)
+        load_x(2)
         load_d4_pooled(0)
-        load_x(4)
+        load_x(3)
         for k in range(1, len(DT_PIECES)):
             load_dt(k)
         load_d4_pooled(1)

import concourse.mybir as mybir
from concourse.masks import make_identity

F32 = mybir.dt.float32
BF16 = mybir.dt.bfloat16
U16 = mybir.dt.uint16
COPY = mybir.ActivationFunctionType.Copy
RELU = mybir.ActivationFunctionType.Relu

P = 128
CHANNELS = 1024
POINTS = 1024
LISTED = 512
NEIGHBOURS = 4
SAMPLED = LISTED // NEIGHBOURS
OUT_CHANNELS = 512
SLOTS = CHANNELS // P
OUT_SLOTS = OUT_CHANNELS // P
VECTOR_ROWS = 64
DMA_STEP = 256
BANK = 512
PER_BANK = BANK // SAMPLED
X_PIECES = (2, 4, 1, 1)
X_FIRST = tuple(sum(X_PIECES[:k]) for k in range(len(X_PIECES)))
DT_PIECES = (4, 2, 2)
DT_FIRST = tuple(sum(DT_PIECES[:k]) for k in range(len(DT_PIECES)))
D4_POOLED_PIECE = 4
OUT_HALF = OUT_SLOTS // 2
D4_H_PIECES = ((0, 4, 0, OUT_SLOTS), (4, 2, 0, OUT_SLOTS), (6, 2, 0, OUT_HALF), (6, 2, OUT_HALF, OUT_HALF))

FLOPS = 2 * SAMPLED * (CHANNELS * CHANNELS + 2 * CHANNELS * OUT_CHANNELS)


def tile_c3dnet_kernel(tc, x, dt_w, dt_gain, dt_bias, d4_w, d4_gain, d4_bias, offs, out):
    nc = tc.nc
    with (
        tc.tile_pool(name="held", bufs=1) as held,
        tc.tile_pool(name="ring", bufs=3) as ring,
        tc.psum_pool(name="psum", bufs=1) as psum,
    ):
        offsets = held.tile([P, LISTED // 16], U16, name="offsets")

        x_by_slot = x.rearrange("(p r) s -> p r s", r=SLOTS)
        dt_by_slot = dt_w.rearrange("(p r) m -> p r m", r=SLOTS)
        d4_h_by_slot = d4_w[0:CHANNELS, :].rearrange("(r p) o -> p r o", p=P)
        d4_pooled_by_slot = d4_w[CHANNELS : 2 * CHANNELS, :].rearrange("(p r) o -> p r o", r=SLOTS)

        x_pieces = [held.tile([P, slots, POINTS], F32, name=f"x{k}", align_bytes=DMA_STEP) for k, slots in enumerate(X_PIECES)]
        x_windows = [x_pieces[k][:, j, :] for k, slots in enumerate(X_PIECES) for j in range(slots)]
        dt_pieces = [held.tile([P, slots, CHANNELS], BF16, name=f"dt{k}", align_bytes=DMA_STEP) for k, slots in enumerate(DT_PIECES)]
        dt_rows = [dt_pieces[k][:, j, :] for k, slots in enumerate(DT_PIECES) for j in range(slots)]
        d4_pooled_pieces = [
            held.tile([P, D4_POOLED_PIECE, OUT_CHANNELS], BF16, name=f"d4_pooled{k}", align_bytes=DMA_STEP)
            for k in range(SLOTS // D4_POOLED_PIECE)
        ]
        d4_h_pieces = [
            held.tile([P, slots, out_slots * P], BF16, name=f"d4_h{k}", align_bytes=DMA_STEP)
            for k, (first, slots, out_first, out_slots) in enumerate(D4_H_PIECES)
        ]

        vector_rows = held.tile([VECTOR_ROWS, P], F32, name="vector_rows", align_bytes=DMA_STEP)
        nc.vector.memset(vector_rows[:], 0.0)
        vectors = (dt_gain, dt_bias, d4_gain, d4_bias)
        vector_slots = (SLOTS, SLOTS, OUT_SLOTS, OUT_SLOTS)
        vector_first = [sum(vector_slots[:k]) for k in range(len(vectors))]

        def load_vector(k):
            rows = vector_rows[vector_first[k] : vector_first[k] + vector_slots[k], :]
            nc.sync.dma_start(rows, vectors[k].rearrange("(r p) one -> r (p one)", p=P))

        def load_x(k):
            nc.sync.dma_start(x_pieces[k][:], x_by_slot[:, X_FIRST[k] : X_FIRST[k] + X_PIECES[k], :])

        def load_dt(k):
            nc.sync.dma_start(dt_pieces[k][:], dt_by_slot[:, DT_FIRST[k] : DT_FIRST[k] + DT_PIECES[k], :])

        def load_d4_pooled(k):
            nc.sync.dma_start(
                d4_pooled_pieces[k][:], d4_pooled_by_slot[:, k * D4_POOLED_PIECE : (k + 1) * D4_POOLED_PIECE, :]
            )

        def load_d4_h(k):
            first, slots, out_first, out_slots = D4_H_PIECES[k]
            nc.sync.dma_start(
                d4_h_pieces[k][:],
                d4_h_by_slot[:, first : first + slots, out_first * P : (out_first + out_slots) * P],
            )

        load_x(0)
        nc.sync.dma_start(offsets[:], offs)
        for k in range(len(vectors)):
            load_vector(k)
        load_x(1)
        load_dt(0)
        load_x(2)
        load_d4_pooled(0)
        load_x(3)
        for k in range(1, len(DT_PIECES)):
            load_dt(k)
        load_d4_pooled(1)
        for k in range(len(D4_H_PIECES)):
            load_d4_h(k)

        def block(rows, k):
            return rows[:, k * P : (k + 1) * P]

        def dt_weights(r_in, r_out):
            return block(dt_rows[r_in], r_out)

        def d4_pooled_weights(r_in, q_out):
            rows = d4_pooled_pieces[r_in // D4_POOLED_PIECE][:, r_in % D4_POOLED_PIECE, :]
            return block(rows, q_out)

        identity = held.tile([VECTOR_ROWS, VECTOR_ROWS], F32, name="identity")
        make_identity(nc, identity[:])
        flipped = psum.tile([P, VECTOR_ROWS], F32, name="flipped")
        nc.tensor.transpose(flipped[:], vector_rows[:], identity[:])
        vector_columns = held.tile([P, sum(vector_slots)], F32, name="vector_columns")
        nc.vector.tensor_copy(vector_columns[:], flipped[:, 0 : sum(vector_slots)])
        dt_gains, dt_biases, d4_gains, d4_biases = [
            vector_columns[:, first : first + slots] for first, slots in zip(vector_first, vector_slots)
        ]

        zeros = held.tile([P, BANK], BF16, name="zeros")
        nc.scalar.memzero(zeros[:])
        h_banks = [psum.tile([P, BANK], F32, name=f"h_bank{b}") for b in range(SLOTS // PER_BANK)]
        for bank in h_banks:
            nc.tensor.matmul(bank[:], zeros[:, 0:P], zeros[:], start=True, stop=False)

        def h_sum(r):
            return h_banks[r // PER_BANK][:, (r % PER_BANK) * SAMPLED : (r % PER_BANK + 1) * SAMPLED]

        out_sums = [psum.tile([P, SAMPLED], F32, name=f"out_sum{q}") for q in range(OUT_SLOTS)]

        pooled = [held.tile([P, SAMPLED], BF16, name=f"pooled{r}") for r in range(SLOTS)]

        def pool(r):
            picked = ring.tile([P, LISTED], F32, name="picked")
            nc.scalar.activation(picked[:], x_windows[r].indirect(offsets[:]), COPY)
            with nc.allow_low_precision(reason="a maximum is one of its inputs: the only rounding is the asked one to bfloat16"):
                nc.vector.tensor_reduce(
                    pooled[r][:],
                    picked[:].rearrange("p (n t) -> p n t", t=NEIGHBOURS),
                    axis=mybir.AxisListType.X,
                    op=mybir.AluOpType.max,
                )

        def first_convolution(r_in):
            for r_out in range(SLOTS):
                nc.tensor.matmul(
                    h_sum(r_out),
                    dt_weights(r_in, r_out),
                    pooled[r_in][:],
                    start=False,
                    stop=(r_in == SLOTS - 1 and r_out % PER_BANK == PER_BANK - 1),
                )

        def pooled_share(r_in):
            for q_out in range(OUT_SLOTS):
                nc.tensor.matmul(
                    out_sums[q_out][:], d4_pooled_weights(r_in, q_out), pooled[r_in][:], start=(r_in == 0), stop=False
                )

        for r in range(SLOTS):
            pool(r)
        for r_in in range(D4_POOLED_PIECE):
            first_convolution(r_in)
        for r_in in range(D4_POOLED_PIECE):
            pooled_share(r_in)
        for r_in in range(D4_POOLED_PIECE, SLOTS):
            first_convolution(r_in)
        for r_in in range(D4_POOLED_PIECE, SLOTS):
            pooled_share(r_in)

        h = [held.tile([P, SAMPLED], BF16, name=f"h{r}") for r in range(SLOTS)]
        for r in range(SLOTS):
            nc.scalar.activation(h[r][:], h_sum(r), RELU, bias=dt_biases[:, r : r + 1], scale=dt_gains[:, r : r + 1])
        out_by_slot = out.rearrange("(q p) n -> p q n", p=P)
        result = held.tile([P, OUT_SLOTS, SAMPLED], F32, name="result", align_bytes=DMA_STEP)

        def finish(q):
            gain, bias = d4_gains[:, q : q + 1], d4_biases[:, q : q + 1]
            nc.scalar.activation(result[:, q, :], out_sums[q][:], RELU, bias=bias, scale=gain)
            queue = nc.sync if q % 2 == 0 else nc.scalar
            queue.dma_start(out_by_slot[:, q, :], result[:, q, :])

        for k, (first, slots, out_first, out_slots) in enumerate(D4_H_PIECES):
            for q_out in range(out_first, out_first + out_slots):
                for r_in in range(first, first + slots):
                    nc.tensor.matmul(
                        out_sums[q_out][:],
                        block(d4_h_pieces[k][:, r_in - first, :], q_out - out_first),
                        h[r_in][:],
                        start=False,
                        stop=(r_in == SLOTS - 1),
                    )
                if first + slots == SLOTS:
                    finish(q_out)
